import numpy as np
import ml_dtypes

BF16 = ml_dtypes.bfloat16


def bf(x):
    return np.asarray(x, np.float32).astype(BF16)


def f32(x):
    return np.asarray(x, np.float32)


def f64(x):
    return np.asarray(x).astype(np.float64)


def striped(idx):
    return np.tile(idx.reshape(-1, 16).T, (8, 1))


E, M, C, S, N, T = 2, 256, 512, 256, 512, 512
ZP, LEVELS = 8.0, 16
LO, HI = 0.01, 0.05


def setup_inputs():
    return {"scale": f32(np.random.uniform(LO, HI, (C, S))), "q": f32(np.random.choice(LEVELS, (C, N))), "state": bf(np.random.standard_normal((N, E * T))), "offs": striped(np.random.permutation(np.tile(np.arange(S), 2))[:N])}


def reference(scale, q, state, offs):
    idx = offs[:16].T.reshape(-1)
    wt = (f64(q) - ZP) * f64(scale)[:, idx]
    st = f64(state)
    return np.concatenate([wt[e * M:(e + 1) * M] @ st[:, e * T:(e + 1) * T] for e in range(E)], axis=1)

@@ -1,0 +1,77 @@
+import concourse.masks as masks
+import concourse.mybir as mybir
+
+F32, BF16, U16 = mybir.dt.float32, mybir.dt.bfloat16, mybir.dt.uint16
+MULT = mybir.AluOpType.mult
+COPY = mybir.ActivationFunctionType.Copy
+
+P = 128
+EXPERTS, M, T = 2, 256, 512
+GROUPS = 256
+N = 512
+ZERO_POINT = 8.0
+PIECE = 256
+ROW_BLOCKS = EXPERTS * M // P
+J_BLOCKS = N // P
+FLOPS = 2 * EXPERTS * M * N * T
+
+
+def tile_moewna16matmul_kernel(tc, scale, q, state, offs, out):
+    nc = tc.nc
+    with (
+        tc.tile_pool(name="held", bufs=1) as held,
+        tc.psum_pool(name="psum", bufs=1) as psum,
+    ):
+        offsets = held.tile([P, N // 16], U16, name="offsets")
+        nc.sync.dma_start(offsets[:], offs)
+        scale_sb, q_sb, state_sb = [], [], []
+        for b in range(ROW_BLOCKS):
+            rows = slice(b * P, (b + 1) * P)
+            scale_sb.append(held.tile([P, GROUPS], F32, name=f"scale{b}"))
+            nc.sync.dma_start(scale_sb[b][:], scale[rows, :])
+            q_sb.append(held.tile([P, N], F32, name=f"q{b}"))
+            nc.sync.dma_start(q_sb[b][:], q[rows, :])
+        for k in range(J_BLOCKS):
+            state_sb.append(held.tile([P, EXPERTS * T], BF16, name=f"state{k}"))
+            nc.scalar.dma_start(state_sb[k][:], state[k * P : (k + 1) * P, :])
+
+        identity = held.tile([P, P], F32, name="identity")
+        masks.make_identity(nc, identity[:])
+
+        for b in range(ROW_BLOCKS):
+            expert, m_block = divmod(b, M // P)
+
+            centred = held.tile([P, N], F32, name=f"centred{b}")
+            nc.scalar.activation(centred[:], q_sb[b][:], COPY, bias=-ZERO_POINT)
+
+            wt = held.tile([P, N], F32, name=f"wt{b}")
+            for j0 in range(0, N, PIECE):
+                nc.vector.tensor_tensor(
+                    wt[:, j0 : j0 + PIECE],
+                    scale_sb[b][:].indirect(offsets[:, j0 // 16 : (j0 + PIECE) // 16]),
+                    centred[:, j0 : j0 + PIECE],
+                    MULT,
+                )
+
+            flipped = psum.tile([P, N], F32, name=f"flipped{b}")
+            for k in range(J_BLOCKS):
+                cols = slice(k * P, (k + 1) * P)
+                nc.tensor.transpose(flipped[:, cols], wt[:, cols], identity[:])
+
+            wt_t = held.tile([P, N], BF16, name=f"wt_t{b}")
+            nc.scalar.activation(wt_t[:], flipped[:], COPY)
+
+            tokens = slice(expert * T, (expert + 1) * T)
+            acc = psum.tile([P, T], F32, name=f"acc{b}")
+            for k in range(J_BLOCKS):
+                nc.tensor.matmul(
+                    acc[:],
+                    wt_t[:, k * P : (k + 1) * P],
+                    state_sb[k][:, tokens],
+                    start=(k == 0),
+                    stop=(k == J_BLOCKS - 1),
+                )
+
+            result = held.tile([P, T], F32, name=f"result{b}")
+            nc.vector.tensor_copy(result[:], acc[:])
+            nc.sync.dma_start(out[m_block * P : (m_block + 1) * P, tokens], result[:])

@@ -11,6 +11,7 @@ GROUPS = 256
 N = 512
 ZERO_POINT = 8.0
 PIECE = 256
+PIECES = N // PIECE
 ROW_BLOCKS = EXPERTS * M // P
 J_BLOCKS = N // P
 FLOPS = 2 * EXPERTS * M * N * T
@@ -20,58 +21,67 @@ def tile_moewna16matmul_kernel(tc, scale, q, state, offs, out):
     nc = tc.nc
     with (
         tc.tile_pool(name="held", bufs=1) as held,
-        tc.psum_pool(name="psum", bufs=1) as psum,
+        tc.psum_pool(name="flip", bufs=4) as flip,
+        tc.psum_pool(name="accs", bufs=4) as accs,
     ):
         offsets = held.tile([P, N // 16], U16, name="offsets")
         nc.sync.dma_start(offsets[:], offs)
-        scale_sb, q_sb, state_sb = [], [], []
-        for b in range(ROW_BLOCKS):
-            rows = slice(b * P, (b + 1) * P)
-            scale_sb.append(held.tile([P, GROUPS], F32, name=f"scale{b}"))
-            nc.sync.dma_start(scale_sb[b][:], scale[rows, :])
-            q_sb.append(held.tile([P, N], F32, name=f"q{b}"))
-            nc.sync.dma_start(q_sb[b][:], q[rows, :])
-        for k in range(J_BLOCKS):
-            state_sb.append(held.tile([P, EXPERTS * T], BF16, name=f"state{k}"))
-            nc.scalar.dma_start(state_sb[k][:], state[k * P : (k + 1) * P, :])
+        scale_sb = [held.tile([P, GROUPS], F32, name=f"scale{b}") for b in range(ROW_BLOCKS)]
+        q_sb = [
+            [held.tile([P, PIECE], F32, name=f"q{b}_{h}") for h in range(PIECES)] for b in range(ROW_BLOCKS)
+        ]
+        state_sb = [
+            [held.tile([P, T], BF16, name=f"state{e}_{k}") for k in range(J_BLOCKS)] for e in range(EXPERTS)
+        ]
+        for e in range(EXPERTS):
+            for b in range(e * M // P, (e + 1) * M // P):
+                rows = slice(b * P, (b + 1) * P)
+                nc.sync.dma_start(q_sb[b][0][:], q[rows, 0:PIECE])
+                nc.sync.dma_start(scale_sb[b][:], scale[rows, :])
+                for h in range(1, PIECES):
+                    nc.sync.dma_start(q_sb[b][h][:], q[rows, h * PIECE : (h + 1) * PIECE])
+            for k in range(J_BLOCKS):
+                nc.sync.dma_start(state_sb[e][k][:], state[k * P : (k + 1) * P, e * T : (e + 1) * T])
 
         identity = held.tile([P, P], F32, name="identity")
         masks.make_identity(nc, identity[:])
 
         for b in range(ROW_BLOCKS):
-            expert, m_block = divmod(b, M // P)
+            e, m_block = divmod(b, M // P)
+            acc = accs.tile([P, T], F32, name="acc")
+            for h in range(PIECES):
+                centred = held.tile([P, PIECE], F32, name=f"centred{b}_{h}")
+                nc.scalar.activation(centred[:], q_sb[b][h][:], COPY, bias=-ZERO_POINT)
 
-            centred = held.tile([P, N], F32, name=f"centred{b}")
-            nc.scalar.activation(centred[:], q_sb[b][:], COPY, bias=-ZERO_POINT)
-
-            wt = held.tile([P, N], F32, name=f"wt{b}")
-            for j0 in range(0, N, PIECE):
+                wt = held.tile([P, PIECE], F32, name=f"wt{b}_{h}")
                 nc.vector.tensor_tensor(
-                    wt[:, j0 : j0 + PIECE],
-                    scale_sb[b][:].indirect(offsets[:, j0 // 16 : (j0 + PIECE) // 16]),
-                    centred[:, j0 : j0 + PIECE],
+                    wt[:],
+                    scale_sb[b][:].indirect(offsets[:, h * PIECE // 16 : (h + 1) * PIECE // 16]),
+                    centred[:],
                     MULT,
                 )
 
-            flipped = psum.tile([P, N], F32, name=f"flipped{b}")
-            for k in range(J_BLOCKS):
-                cols = slice(k * P, (k + 1) * P)
-                nc.tensor.transpose(flipped[:, cols], wt[:, cols], identity[:])
+                flipped = flip.tile([P, PIECE], F32, name="flipped")
+                for i in range(PIECE // P):
+                    cols = slice(i * P, (i + 1) * P)
+                    nc.tensor.transpose(flipped[:, cols], wt[:, cols], identity[:])
 
-            wt_t = held.tile([P, N], BF16, name=f"wt_t{b}")
-            nc.scalar.activation(wt_t[:], flipped[:], COPY)
+                wt_t = held.tile([P, PIECE], BF16, name=f"wt_t{b}_{h}")
+                nc.scalar.activation(wt_t[:], flipped[:], COPY)
 
-            tokens = slice(expert * T, (expert + 1) * T)
-            acc = psum.tile([P, T], F32, name=f"acc{b}")
-            for k in range(J_BLOCKS):
-                nc.tensor.matmul(
-                    acc[:],
-                    wt_t[:, k * P : (k + 1) * P],
-                    state_sb[k][:, tokens],
-                    start=(k == 0),
-                    stop=(k == J_BLOCKS - 1),
-                )
+                for i in range(PIECE // P):
+                    k = h * PIECE // P + i
+                    nc.tensor.matmul(
+                        acc[:],
+                        wt_t[:, i * P : (i + 1) * P],
+                        state_sb[e][k][:],
+                        start=(k == 0),
+                        stop=(k == J_BLOCKS - 1),
+                    )
 
             result = held.tile([P, T], F32, name=f"result{b}")
-            nc.vector.tensor_copy(result[:], acc[:])
-            nc.sync.dma_start(out[m_block * P : (m_block + 1) * P, tokens], result[:])
+            if e == 0:
+                nc.scalar.activation(result[:], acc[:], COPY)
+            else:
+                nc.vector.tensor_copy(result[:], acc[:])
+            nc.sync.dma_start(out[m_block * P : (m_block + 1) * P, e * T : (e + 1) * T], result[:])

@@ -14,6 +14,7 @@ PIECE = 256
 PIECES = N // PIECE
 ROW_BLOCKS = EXPERTS * M // P
 J_BLOCKS = N // P
+WARM_UP = 5
 FLOPS = 2 * EXPERTS * M * N * T
 
 
@@ -21,8 +22,9 @@ def tile_moewna16matmul_kernel(tc, scale, q, state, offs, out):
     nc = tc.nc
     with (
         tc.tile_pool(name="held", bufs=1) as held,
-        tc.psum_pool(name="flip", bufs=4) as flip,
+        tc.psum_pool(name="flip", bufs=3) as flip,
         tc.psum_pool(name="accs", bufs=4) as accs,
+        tc.psum_pool(name="idle", bufs=1) as idle,
     ):
         offsets = held.tile([P, N // 16], U16, name="offsets")
         nc.sync.dma_start(offsets[:], offs)
@@ -42,6 +44,12 @@ def tile_moewna16matmul_kernel(tc, scale, q, state, offs, out):
                     nc.sync.dma_start(q_sb[b][h][:], q[rows, h * PIECE : (h + 1) * PIECE])
             for k in range(J_BLOCKS):
                 nc.sync.dma_start(state_sb[e][k][:], state[k * P : (k + 1) * P, e * T : (e + 1) * T])
+
+        zeros = held.tile([P, T], BF16, name="zeros")
+        nc.gpsimd.memset(zeros[:], 0.0)
+        unused = idle.tile([P, T], F32, name="unused")
+        for i in range(WARM_UP):
+            nc.tensor.matmul(unused[:], zeros[:, 0:P], zeros[:], start=True, stop=True)
 
         identity = held.tile([P, P], F32, name="identity")
         masks.make_identity(nc, identity[:])

@@ -73,6 +73,7 @@ def tile_moewna16matmul_kernel(tc, scale, q, state, offs, out):
                 for i in range(PIECE // P):
                     cols = slice(i * P, (i + 1) * P)
                     nc.tensor.transpose(flipped[:, cols], wt[:, cols], identity[:])
+                nc.tensor.matmul(unused[:], zeros[:, 0:P], zeros[:], start=True, stop=True)
 
                 wt_t = held.tile([P, PIECE], BF16, name=f"wt_t{b}_{h}")
                 nc.scalar.activation(wt_t[:], flipped[:], COPY)

@@ -73,7 +73,8 @@ def tile_moewna16matmul_kernel(tc, scale, q, state, offs, out):
                 for i in range(PIECE // P):
                     cols = slice(i * P, (i + 1) * P)
                     nc.tensor.transpose(flipped[:, cols], wt[:, cols], identity[:])
-                nc.tensor.matmul(unused[:], zeros[:, 0:P], zeros[:], start=True, stop=True)
+                if m_block == 0:
+                    nc.tensor.matmul(unused[:], zeros[:, 0:P], zeros[:], start=True, stop=True)
 
                 wt_t = held.tile([P, PIECE], BF16, name=f"wt_t{b}_{h}")
                 nc.scalar.activation(wt_t[:], flipped[:], COPY)

@@ -14,7 +14,8 @@ PIECE = 256
 PIECES = N // PIECE
 ROW_BLOCKS = EXPERTS * M // P
 J_BLOCKS = N // P
-WARM_UP = 5
+WARM_UP = 7
+KEEP_UP = 2
 FLOPS = 2 * EXPERTS * M * N * T
 
 
@@ -73,11 +74,13 @@ def tile_moewna16matmul_kernel(tc, scale, q, state, offs, out):
                 for i in range(PIECE // P):
                     cols = slice(i * P, (i + 1) * P)
                     nc.tensor.transpose(flipped[:, cols], wt[:, cols], identity[:])
-                if m_block == 0:
-                    nc.tensor.matmul(unused[:], zeros[:, 0:P], zeros[:], start=True, stop=True)
 
                 wt_t = held.tile([P, PIECE], BF16, name=f"wt_t{b}_{h}")
                 nc.scalar.activation(wt_t[:], flipped[:], COPY)
+
+                if m_block == 0 and h == 0:
+                    for i in range(KEEP_UP):
+                        nc.tensor.matmul(unused[:], wt_t[:, 0:P], zeros[:], start=True, stop=True)
 
                 for i in range(PIECE // P):
                     k = h * PIECE // P + i

@@ -12,10 +12,11 @@ N = 512
 ZERO_POINT = 8.0
 PIECE = 256
 PIECES = N // PIECE
-ROW_BLOCKS = EXPERTS * M // P
+M_BLOCKS = M // P
+ROW_BLOCKS = EXPERTS * M_BLOCKS
 J_BLOCKS = N // P
-WARM_UP = 7
-KEEP_UP = 2
+HALF = T // 2
+WARM_UP = 13
 FLOPS = 2 * EXPERTS * M * N * T
 
 
@@ -24,7 +25,7 @@ def tile_moewna16matmul_kernel(tc, scale, q, state, offs, out):
     with (
         tc.tile_pool(name="held", bufs=1) as held,
         tc.psum_pool(name="flip", bufs=3) as flip,
-        tc.psum_pool(name="accs", bufs=4) as accs,
+        tc.psum_pool(name="sums", bufs=ROW_BLOCKS) as sums,
         tc.psum_pool(name="idle", bufs=1) as idle,
     ):
         offsets = held.tile([P, N // 16], U16, name="offsets")
@@ -37,7 +38,7 @@ def tile_moewna16matmul_kernel(tc, scale, q, state, offs, out):
             [held.tile([P, T], BF16, name=f"state{e}_{k}") for k in range(J_BLOCKS)] for e in range(EXPERTS)
         ]
         for e in range(EXPERTS):
-            for b in range(e * M // P, (e + 1) * M // P):
+            for b in range(e * M_BLOCKS, (e + 1) * M_BLOCKS):
                 rows = slice(b * P, (b + 1) * P)
                 nc.sync.dma_start(q_sb[b][0][:], q[rows, 0:PIECE])
                 nc.sync.dma_start(scale_sb[b][:], scale[rows, :])
@@ -56,8 +57,8 @@ def tile_moewna16matmul_kernel(tc, scale, q, state, offs, out):
         masks.make_identity(nc, identity[:])
 
         for b in range(ROW_BLOCKS):
-            e, m_block = divmod(b, M // P)
-            acc = accs.tile([P, T], F32, name="acc")
+            e, m_block = divmod(b, M_BLOCKS)
+            acc = sums.tile([P, T], F32, name="acc")
             for h in range(PIECES):
                 centred = held.tile([P, PIECE], F32, name=f"centred{b}_{h}")
                 nc.scalar.activation(centred[:], q_sb[b][h][:], COPY, bias=-ZERO_POINT)
@@ -78,10 +79,6 @@ def tile_moewna16matmul_kernel(tc, scale, q, state, offs, out):
                 wt_t = held.tile([P, PIECE], BF16, name=f"wt_t{b}_{h}")
                 nc.scalar.activation(wt_t[:], flipped[:], COPY)
 
-                if m_block == 0 and h == 0:
-                    for i in range(KEEP_UP):
-                        nc.tensor.matmul(unused[:], wt_t[:, 0:P], zeros[:], start=True, stop=True)
-
                 for i in range(PIECE // P):
                     k = h * PIECE // P + i
                     nc.tensor.matmul(
@@ -92,9 +89,12 @@ def tile_moewna16matmul_kernel(tc, scale, q, state, offs, out):
                         stop=(k == J_BLOCKS - 1),
                     )
 
-            result = held.tile([P, T], F32, name=f"result{b}")
-            if e == 0:
-                nc.scalar.activation(result[:], acc[:], COPY)
-            else:
-                nc.vector.tensor_copy(result[:], acc[:])
-            nc.sync.dma_start(out[m_block * P : (m_block + 1) * P, e * T : (e + 1) * T], result[:])
+            for t0 in range(0, T, HALF):
+                result = held.tile([P, HALF], F32, name=f"result{b}_{t0}")
+                if e == 0:
+                    nc.scalar.activation(result[:], acc[:, t0 : t0 + HALF], COPY)
+                else:
+                    nc.vector.tensor_copy(result[:], acc[:, t0 : t0 + HALF])
+                nc.sync.dma_start(
+                    out[m_block * P : (m_block + 1) * P, e * T + t0 : e * T + t0 + HALF], result[:]
+                )

@@ -25,7 +25,7 @@ def tile_moewna16matmul_kernel(tc, scale, q, state, offs, out):
     with (
         tc.tile_pool(name="held", bufs=1) as held,
         tc.psum_pool(name="flip", bufs=3) as flip,
-        tc.psum_pool(name="sums", bufs=ROW_BLOCKS) as sums,
+        tc.psum_pool(name="sums", bufs=4) as sums,
         tc.psum_pool(name="idle", bufs=1) as idle,
     ):
         offsets = held.tile([P, N // 16], U16, name="offsets")
@@ -58,7 +58,9 @@ def tile_moewna16matmul_kernel(tc, scale, q, state, offs, out):
 
         for b in range(ROW_BLOCKS):
             e, m_block = divmod(b, M_BLOCKS)
-            acc = sums.tile([P, T], F32, name="acc")
+            last_block = b == ROW_BLOCKS - 1
+            width = HALF if last_block else T
+            acc = {t0: sums.tile([P, width], F32, name="acc") for t0 in range(0, T, width)}
             for h in range(PIECES):
                 centred = held.tile([P, PIECE], F32, name=f"centred{b}_{h}")
                 nc.scalar.activation(centred[:], q_sb[b][h][:], COPY, bias=-ZERO_POINT)
@@ -81,20 +83,22 @@ def tile_moewna16matmul_kernel(tc, scale, q, state, offs, out):
 
                 for i in range(PIECE // P):
                     k = h * PIECE // P + i
-                    nc.tensor.matmul(
-                        acc[:],
-                        wt_t[:, i * P : (i + 1) * P],
-                        state_sb[e][k][:],
-                        start=(k == 0),
-                        stop=(k == J_BLOCKS - 1),
-                    )
+                    for t0 in acc:
+                        nc.tensor.matmul(
+                            acc[t0][:],
+                            wt_t[:, i * P : (i + 1) * P],
+                            state_sb[e][k][:, t0 : t0 + width],
+                            start=(k == 0),
+                            stop=(k == J_BLOCKS - 1),
+                        )
 
             for t0 in range(0, T, HALF):
                 result = held.tile([P, HALF], F32, name=f"result{b}_{t0}")
-                if e == 0:
-                    nc.scalar.activation(result[:], acc[:, t0 : t0 + HALF], COPY)
+                sums_half = acc[t0][:] if last_block else acc[0][:, t0 : t0 + HALF]
+                if e == 0 or (last_block and t0 == 0):
+                    nc.scalar.activation(result[:], sums_half, COPY)
                 else:
-                    nc.vector.tensor_copy(result[:], acc[:, t0 : t0 + HALF])
+                    nc.vector.tensor_copy(result[:], sums_half)
                 nc.sync.dma_start(
                     out[m_block * P : (m_block + 1) * P, e * T + t0 : e * T + t0 + HALF], result[:]
                 )

@@ -79,7 +79,9 @@ def tile_moewna16matmul_kernel(tc, scale, q, state, offs, out):
                     nc.tensor.transpose(flipped[:, cols], wt[:, cols], identity[:])
 
                 wt_t = held.tile([P, PIECE], BF16, name=f"wt_t{b}_{h}")
-                nc.scalar.activation(wt_t[:], flipped[:], COPY)
+                for i in range(PIECE // P):
+                    cols = slice(i * P, (i + 1) * P)
+                    nc.scalar.activation(wt_t[:, cols], flipped[:, cols], COPY)
 
                 for i in range(PIECE // P):
                     k = h * PIECE // P + i

@@ -16,7 +16,7 @@ M_BLOCKS = M // P
 ROW_BLOCKS = EXPERTS * M_BLOCKS
 J_BLOCKS = N // P
 HALF = T // 2
-WARM_UP = 13
+WARM_UP = 12
 FLOPS = 2 * EXPERTS * M * N * T
 
 

@@ -15,8 +15,10 @@ PIECES = N // PIECE
 M_BLOCKS = M // P
 ROW_BLOCKS = EXPERTS * M_BLOCKS
 J_BLOCKS = N // P
+J_PER_PIECE = PIECE // P
 HALF = T // 2
-WARM_UP = 12
+WARM_UP = 10
+Q_AHEAD = 2
 FLOPS = 2 * EXPERTS * M * N * T
 
 
@@ -32,20 +34,38 @@ def tile_moewna16matmul_kernel(tc, scale, q, state, offs, out):
         nc.sync.dma_start(offsets[:], offs)
         scale_sb = [held.tile([P, GROUPS], F32, name=f"scale{b}") for b in range(ROW_BLOCKS)]
         q_sb = [
-            [held.tile([P, PIECE], F32, name=f"q{b}_{h}") for h in range(PIECES)] for b in range(ROW_BLOCKS)
+            [
+                held.tile([P, PIECE], F32, name=f"q{b}_{h}", tag=f"piece{PIECES * b + h}")
+                for h in range(PIECES)
+            ]
+            for b in range(ROW_BLOCKS)
         ]
         state_sb = [
             [held.tile([P, T], BF16, name=f"state{e}_{k}") for k in range(J_BLOCKS)] for e in range(EXPERTS)
         ]
-        for e in range(EXPERTS):
-            for b in range(e * M_BLOCKS, (e + 1) * M_BLOCKS):
-                rows = slice(b * P, (b + 1) * P)
-                nc.sync.dma_start(q_sb[b][0][:], q[rows, 0:PIECE])
-                nc.sync.dma_start(scale_sb[b][:], scale[rows, :])
-                for h in range(1, PIECES):
-                    nc.sync.dma_start(q_sb[b][h][:], q[rows, h * PIECE : (h + 1) * PIECE])
-            for k in range(J_BLOCKS):
-                nc.sync.dma_start(state_sb[e][k][:], state[k * P : (k + 1) * P, e * T : (e + 1) * T])
+
+        def load_q(b, h):
+            nc.sync.dma_start(q_sb[b][h][:], q[b * P : (b + 1) * P, h * PIECE : (h + 1) * PIECE])
+
+        def load_scale(b):
+            nc.sync.dma_start(scale_sb[b][:], scale[b * P : (b + 1) * P, :])
+
+        def load_state(e, k):
+            nc.sync.dma_start(state_sb[e][k][:], state[k * P : (k + 1) * P, e * T : (e + 1) * T])
+
+        for b in range(ROW_BLOCKS):
+            if b == M_BLOCKS:
+                for k in range(J_PER_PIECE):
+                    load_state(0, k)
+            load_q(b, 0)
+            load_scale(b)
+            if b == M_BLOCKS:
+                load_state(0, J_PER_PIECE)
+            load_q(b, 1)
+            if b == M_BLOCKS:
+                load_state(0, J_PER_PIECE + 1)
+        for k in range(J_BLOCKS):
+            load_state(1, k)
 
         zeros = held.tile([P, T], BF16, name="zeros")
         nc.gpsimd.memset(zeros[:], 0.0)
@@ -56,51 +76,72 @@ def tile_moewna16matmul_kernel(tc, scale, q, state, offs, out):
         identity = held.tile([P, P], F32, name="identity")
         masks.make_identity(nc, identity[:])
 
+        centred = [
+            [held.tile([P, PIECE], F32, name=f"centred{b}_{h}") for h in range(PIECES)] for b in range(ROW_BLOCKS)
+        ]
         for b in range(ROW_BLOCKS):
-            e, m_block = divmod(b, M_BLOCKS)
+            for h in range(PIECES):
+                nc.scalar.activation(centred[b][h][:], q_sb[b][h][:], COPY, bias=-ZERO_POINT)
+
+        acc = {}
+
+        def multiply(weights, b, k):
+            e = b // M_BLOCKS
             last_block = b == ROW_BLOCKS - 1
             width = HALF if last_block else T
-            acc = {t0: sums.tile([P, width], F32, name="acc") for t0 in range(0, T, width)}
-            for h in range(PIECES):
-                centred = held.tile([P, PIECE], F32, name=f"centred{b}_{h}")
-                nc.scalar.activation(centred[:], q_sb[b][h][:], COPY, bias=-ZERO_POINT)
-
-                wt = held.tile([P, PIECE], F32, name=f"wt{b}_{h}")
-                nc.vector.tensor_tensor(
-                    wt[:],
-                    scale_sb[b][:].indirect(offsets[:, h * PIECE // 16 : (h + 1) * PIECE // 16]),
-                    centred[:],
-                    MULT,
+            if k == 0:
+                acc[b] = {t0: sums.tile([P, width], F32, name="acc") for t0 in range(0, T, width)}
+            for t0, bank in acc[b].items():
+                nc.tensor.matmul(
+                    bank[:],
+                    weights,
+                    state_sb[e][k][:, t0 : t0 + width],
+                    start=(k == 0),
+                    stop=(k == J_BLOCKS - 1),
                 )
 
-                flipped = flip.tile([P, PIECE], F32, name="flipped")
-                for i in range(PIECE // P):
-                    cols = slice(i * P, (i + 1) * P)
-                    nc.tensor.transpose(flipped[:, cols], wt[:, cols], identity[:])
-
-                wt_t = held.tile([P, PIECE], BF16, name=f"wt_t{b}_{h}")
-                for i in range(PIECE // P):
-                    cols = slice(i * P, (i + 1) * P)
-                    nc.scalar.activation(wt_t[:, cols], flipped[:, cols], COPY)
-
-                for i in range(PIECE // P):
-                    k = h * PIECE // P + i
-                    for t0 in acc:
-                        nc.tensor.matmul(
-                            acc[t0][:],
-                            wt_t[:, i * P : (i + 1) * P],
-                            state_sb[e][k][:, t0 : t0 + width],
-                            start=(k == 0),
-                            stop=(k == J_BLOCKS - 1),
-                        )
-
+        def store(b):
+            e, m_block = divmod(b, M_BLOCKS)
+            last_block = b == ROW_BLOCKS - 1
             for t0 in range(0, T, HALF):
                 result = held.tile([P, HALF], F32, name=f"result{b}_{t0}")
-                sums_half = acc[t0][:] if last_block else acc[0][:, t0 : t0 + HALF]
-                if e == 0 or (last_block and t0 == 0):
+                sums_half = acc[b][t0][:] if last_block else acc[b][0][:, t0 : t0 + HALF]
+                if last_block and t0 == 0:
                     nc.scalar.activation(result[:], sums_half, COPY)
                 else:
                     nc.vector.tensor_copy(result[:], sums_half)
                 nc.sync.dma_start(
                     out[m_block * P : (m_block + 1) * P, e * T + t0 : e * T + t0 + HALF], result[:]
                 )
+
+        def copy_and_multiply(group, number):
+            flipped, members = group
+            width = len(members) * P
+            wt_t = held.tile([P, width], BF16, name=f"wt_t{number}", tag=f"piece{number + Q_AHEAD}")
+            nc.scalar.activation(wt_t[:], flipped[:, 0:width], COPY)
+            for i, (b, k) in enumerate(members):
+                multiply(wt_t[:, i * P : (i + 1) * P], b, k)
+
+        group = (flip.tile([P, PIECE], F32, name="flipped"), [])
+        for b in range(ROW_BLOCKS):
+            for h in range(PIECES):
+                wt = held.tile([P, PIECE], F32, name=f"wt{b}_{h}")
+                nc.vector.tensor_tensor(
+                    wt[:],
+                    scale_sb[b][:].indirect(offsets[:, h * PIECE // 16 : (h + 1) * PIECE // 16]),
+                    centred[b][h][:],
+                    MULT,
+                )
+
+                full = group
+                group = (flip.tile([P, PIECE], F32, name="flipped"), [])
+                for i, (flipped, members) in enumerate([full, group]):
+                    place = len(members) * P
+                    nc.tensor.transpose(
+                        flipped[:, place : place + P], wt[:, i * P : (i + 1) * P], identity[:]
+                    )
+                    members.append((b, h * J_PER_PIECE + i))
+                copy_and_multiply(full, PIECES * b + h)
+        copy_and_multiply(group, PIECES * ROW_BLOCKS)
+        for b in range(ROW_BLOCKS):
+            store(b)

@@ -17,6 +17,7 @@ ROW_BLOCKS = EXPERTS * M_BLOCKS
 J_BLOCKS = N // P
 J_PER_PIECE = PIECE // P
 HALF = T // 2
+LAST_BANKS = (HALF, HALF // 2, HALF // 2)
 WARM_UP = 10
 Q_AHEAD = 2
 FLOPS = 2 * EXPERTS * M * N * T
@@ -27,8 +28,7 @@ def tile_moewna16matmul_kernel(tc, scale, q, state, offs, out):
     with (
         tc.tile_pool(name="held", bufs=1) as held,
         tc.psum_pool(name="flip", bufs=3) as flip,
-        tc.psum_pool(name="sums", bufs=4) as sums,
-        tc.psum_pool(name="idle", bufs=1) as idle,
+        tc.psum_pool(name="sums", bufs=5) as sums,
     ):
         offsets = held.tile([P, N // 16], U16, name="offsets")
         nc.sync.dma_start(offsets[:], offs)
@@ -69,7 +69,7 @@ def tile_moewna16matmul_kernel(tc, scale, q, state, offs, out):
 
         zeros = held.tile([P, T], BF16, name="zeros")
         nc.gpsimd.memset(zeros[:], 0.0)
-        unused = idle.tile([P, T], F32, name="unused")
+        unused = flip.tile([P, T], F32, name="unused", tag="flipped")
         for i in range(WARM_UP):
             nc.tensor.matmul(unused[:], zeros[:, 0:P], zeros[:], start=True, stop=True)
 
@@ -85,34 +85,29 @@ def tile_moewna16matmul_kernel(tc, scale, q, state, offs, out):
 
         acc = {}
 
-        def multiply(weights, b, k):
-            e = b // M_BLOCKS
-            last_block = b == ROW_BLOCKS - 1
-            width = HALF if last_block else T
-            if k == 0:
-                acc[b] = {t0: sums.tile([P, width], F32, name="acc") for t0 in range(0, T, width)}
-            for t0, bank in acc[b].items():
-                nc.tensor.matmul(
-                    bank[:],
-                    weights,
-                    state_sb[e][k][:, t0 : t0 + width],
-                    start=(k == 0),
-                    stop=(k == J_BLOCKS - 1),
-                )
+        def multiply(bank, weights, e, k, t0, width):
+            nc.tensor.matmul(
+                bank[:],
+                weights,
+                state_sb[e][k][:, t0 : t0 + width],
+                start=(k == 0),
+                stop=(k == J_BLOCKS - 1),
+            )
 
-        def store(b):
+        def copy_and_store(copy_engine, b, t0, sums_part):
             e, m_block = divmod(b, M_BLOCKS)
-            last_block = b == ROW_BLOCKS - 1
-            for t0 in range(0, T, HALF):
-                result = held.tile([P, HALF], F32, name=f"result{b}_{t0}")
-                sums_half = acc[b][t0][:] if last_block else acc[b][0][:, t0 : t0 + HALF]
-                if last_block and t0 == 0:
-                    nc.scalar.activation(result[:], sums_half, COPY)
-                else:
-                    nc.vector.tensor_copy(result[:], sums_half)
-                nc.sync.dma_start(
-                    out[m_block * P : (m_block + 1) * P, e * T + t0 : e * T + t0 + HALF], result[:]
-                )
+            width = sums_part.shape[1]
+            result = held.tile([P, width], F32, name=f"result{b}_{t0}")
+            if copy_engine is nc.scalar:
+                nc.scalar.activation(result[:], sums_part, COPY)
+            else:
+                nc.vector.tensor_copy(result[:], sums_part)
+            nc.sync.dma_start(
+                out[m_block * P : (m_block + 1) * P, e * T + t0 : e * T + t0 + width], result[:]
+            )
+
+        last_block = ROW_BLOCKS - 1
+        last_weights = []
 
         def copy_and_multiply(group, number):
             flipped, members = group
@@ -120,7 +115,13 @@ def tile_moewna16matmul_kernel(tc, scale, q, state, offs, out):
             wt_t = held.tile([P, width], BF16, name=f"wt_t{number}", tag=f"piece{number + Q_AHEAD}")
             nc.scalar.activation(wt_t[:], flipped[:, 0:width], COPY)
             for i, (b, k) in enumerate(members):
-                multiply(wt_t[:, i * P : (i + 1) * P], b, k)
+                weights = wt_t[:, i * P : (i + 1) * P]
+                if b == last_block:
+                    last_weights.append(weights)
+                    continue
+                if k == 0:
+                    acc[b] = sums.tile([P, T], F32, name="acc")
+                multiply(acc[b], weights, b // M_BLOCKS, k, 0, T)
 
         group = (flip.tile([P, PIECE], F32, name="flipped"), [])
         for b in range(ROW_BLOCKS):
@@ -143,5 +144,18 @@ def tile_moewna16matmul_kernel(tc, scale, q, state, offs, out):
                     members.append((b, h * J_PER_PIECE + i))
                 copy_and_multiply(full, PIECES * b + h)
         copy_and_multiply(group, PIECES * ROW_BLOCKS)
-        for b in range(ROW_BLOCKS):
-            store(b)
+
+        parts = []
+        t0 = 0
+        for width in LAST_BANKS:
+            bank = sums.tile([P, width], F32, name="acc")
+            for k, weights in enumerate(last_weights):
+                multiply(bank, weights, EXPERTS - 1, k, t0, width)
+            parts.append((t0, bank[:]))
+            t0 += width
+
+        for b in range(last_block):
+            for t0 in range(0, T, HALF):
+                copy_and_store(nc.vector, b, t0, acc[b][:, t0 : t0 + HALF])
+        for i, (t0, bank) in enumerate(parts):
+            copy_and_store(nc.vector if i % 2 else nc.scalar, last_block, t0, bank)

@@ -18,7 +18,7 @@ J_BLOCKS = N // P
 J_PER_PIECE = PIECE // P
 HALF = T // 2
 LAST_BANKS = (HALF, HALF // 2, HALF // 2)
-WARM_UP = 10
+WARM_UP = 8
 Q_AHEAD = 2
 FLOPS = 2 * EXPERTS * M * N * T
 
@@ -124,6 +124,7 @@ def tile_moewna16matmul_kernel(tc, scale, q, state, offs, out):
                 multiply(acc[b], weights, b // M_BLOCKS, k, 0, T)
 
         group = (flip.tile([P, PIECE], F32, name="flipped"), [])
+        waiting = None
         for b in range(ROW_BLOCKS):
             for h in range(PIECES):
                 wt = held.tile([P, PIECE], F32, name=f"wt{b}_{h}")
@@ -142,7 +143,10 @@ def tile_moewna16matmul_kernel(tc, scale, q, state, offs, out):
                         flipped[:, place : place + P], wt[:, i * P : (i + 1) * P], identity[:]
                     )
                     members.append((b, h * J_PER_PIECE + i))
-                copy_and_multiply(full, PIECES * b + h)
+                if waiting is not None:
+                    copy_and_multiply(*waiting)
+                waiting = (full, PIECES * b + h)
+        copy_and_multiply(*waiting)
         copy_and_multiply(group, PIECES * ROW_BLOCKS)
 
         parts = []

@@ -18,8 +18,8 @@ J_BLOCKS = N // P
 J_PER_PIECE = PIECE // P
 HALF = T // 2
 LAST_BANKS = (HALF, HALF // 2, HALF // 2)
-WARM_UP = 8
-Q_AHEAD = 2
+WARM_UP = 6
+AHEAD = 3
 FLOPS = 2 * EXPERTS * M * N * T
 
 
@@ -34,11 +34,7 @@ def tile_moewna16matmul_kernel(tc, scale, q, state, offs, out):
         nc.sync.dma_start(offsets[:], offs)
         scale_sb = [held.tile([P, GROUPS], F32, name=f"scale{b}") for b in range(ROW_BLOCKS)]
         q_sb = [
-            [
-                held.tile([P, PIECE], F32, name=f"q{b}_{h}", tag=f"piece{PIECES * b + h}")
-                for h in range(PIECES)
-            ]
-            for b in range(ROW_BLOCKS)
+            [held.tile([P, PIECE], F32, name=f"q{b}_{h}") for h in range(PIECES)] for b in range(ROW_BLOCKS)
         ]
         state_sb = [
             [held.tile([P, T], BF16, name=f"state{e}_{k}") for k in range(J_BLOCKS)] for e in range(EXPERTS)
@@ -76,12 +72,15 @@ def tile_moewna16matmul_kernel(tc, scale, q, state, offs, out):
         identity = held.tile([P, P], F32, name="identity")
         masks.make_identity(nc, identity[:])
 
-        centred = [
-            [held.tile([P, PIECE], F32, name=f"centred{b}_{h}") for h in range(PIECES)] for b in range(ROW_BLOCKS)
-        ]
-        for b in range(ROW_BLOCKS):
-            for h in range(PIECES):
-                nc.scalar.activation(centred[b][h][:], q_sb[b][h][:], COPY, bias=-ZERO_POINT)
+        pieces = [(b, h) for b in range(ROW_BLOCKS) for h in range(PIECES)]
+        centred = []
+
+        def subtract_zero_point(u):
+            b, h = pieces[u]
+            tag = f"product{u - AHEAD}" if u >= AHEAD else f"centred{u}"
+            tile_u = held.tile([P, PIECE], F32, name=f"centred{u}", tag=tag)
+            nc.scalar.activation(tile_u[:], q_sb[b][h][:], COPY, bias=-ZERO_POINT)
+            centred.append(tile_u)
 
         acc = {}
 
@@ -112,7 +111,7 @@ def tile_moewna16matmul_kernel(tc, scale, q, state, offs, out):
         def copy_and_multiply(group, number):
             flipped, members = group
             width = len(members) * P
-            wt_t = held.tile([P, width], BF16, name=f"wt_t{number}", tag=f"piece{number + Q_AHEAD}")
+            wt_t = held.tile([P, width], BF16, name=f"wt_t{number}")
             nc.scalar.activation(wt_t[:], flipped[:, 0:width], COPY)
             for i, (b, k) in enumerate(members):
                 weights = wt_t[:, i * P : (i + 1) * P]
@@ -125,29 +124,32 @@ def tile_moewna16matmul_kernel(tc, scale, q, state, offs, out):
 
         group = (flip.tile([P, PIECE], F32, name="flipped"), [])
         waiting = None
-        for b in range(ROW_BLOCKS):
-            for h in range(PIECES):
-                wt = held.tile([P, PIECE], F32, name=f"wt{b}_{h}")
-                nc.vector.tensor_tensor(
-                    wt[:],
-                    scale_sb[b][:].indirect(offsets[:, h * PIECE // 16 : (h + 1) * PIECE // 16]),
-                    centred[b][h][:],
-                    MULT,
-                )
+        for u in range(AHEAD):
+            subtract_zero_point(u)
+        for u, (b, h) in enumerate(pieces):
+            wt = held.tile([P, PIECE], F32, name=f"wt{u}", tag=f"product{u}")
+            nc.vector.tensor_tensor(
+                wt[:],
+                scale_sb[b][:].indirect(offsets[:, h * PIECE // 16 : (h + 1) * PIECE // 16]),
+                centred[u][:],
+                MULT,
+            )
 
-                full = group
-                group = (flip.tile([P, PIECE], F32, name="flipped"), [])
-                for i, (flipped, members) in enumerate([full, group]):
-                    place = len(members) * P
-                    nc.tensor.transpose(
-                        flipped[:, place : place + P], wt[:, i * P : (i + 1) * P], identity[:]
-                    )
-                    members.append((b, h * J_PER_PIECE + i))
-                if waiting is not None:
-                    copy_and_multiply(*waiting)
-                waiting = (full, PIECES * b + h)
+            full = group
+            group = (flip.tile([P, PIECE], F32, name="flipped"), [])
+            for i, (flipped, members) in enumerate([full, group]):
+                place = len(members) * P
+                nc.tensor.transpose(
+                    flipped[:, place : place + P], wt[:, i * P : (i + 1) * P], identity[:]
+                )
+                members.append((b, h * J_PER_PIECE + i))
+            if waiting is not None:
+                copy_and_multiply(*waiting)
+            waiting = (full, u)
+            if u + AHEAD < len(pieces):
+                subtract_zero_point(u + AHEAD)
         copy_and_multiply(*waiting)
-        copy_and_multiply(group, PIECES * ROW_BLOCKS)
+        copy_and_multiply(group, len(pieces))
 
         parts = []
         t0 = 0

import concourse.masks as masks
import concourse.mybir as mybir

F32, BF16, U16 = mybir.dt.float32, mybir.dt.bfloat16, mybir.dt.uint16
MULT = mybir.AluOpType.mult
COPY = mybir.ActivationFunctionType.Copy

P = 128
EXPERTS, M, T = 2, 256, 512
GROUPS = 256
N = 512
ZERO_POINT = 8.0
PIECE = 256
PIECES = N // PIECE
M_BLOCKS = M // P
ROW_BLOCKS = EXPERTS * M_BLOCKS
J_BLOCKS = N // P
J_PER_PIECE = PIECE // P
HALF = T // 2
LAST_BANKS = (HALF, HALF // 2, HALF // 2)
WARM_UP = 6
AHEAD = 3
FLOPS = 2 * EXPERTS * M * N * T


def tile_moewna16matmul_kernel(tc, scale, q, state, offs, out):
    nc = tc.nc
    with (
        tc.tile_pool(name="held", bufs=1) as held,
        tc.psum_pool(name="flip", bufs=3) as flip,
        tc.psum_pool(name="sums", bufs=5) as sums,
    ):
        offsets = held.tile([P, N // 16], U16, name="offsets")
        nc.sync.dma_start(offsets[:], offs)
        scale_sb = [held.tile([P, GROUPS], F32, name=f"scale{b}") for b in range(ROW_BLOCKS)]
        q_sb = [
            [held.tile([P, PIECE], F32, name=f"q{b}_{h}") for h in range(PIECES)] for b in range(ROW_BLOCKS)
        ]
        state_sb = [
            [held.tile([P, T], BF16, name=f"state{e}_{k}") for k in range(J_BLOCKS)] for e in range(EXPERTS)
        ]

        def load_q(b, h):
            nc.sync.dma_start(q_sb[b][h][:], q[b * P : (b + 1) * P, h * PIECE : (h + 1) * PIECE])

        def load_scale(b):
            nc.sync.dma_start(scale_sb[b][:], scale[b * P : (b + 1) * P, :])

        def load_state(e, k):
            nc.sync.dma_start(state_sb[e][k][:], state[k * P : (k + 1) * P, e * T : (e + 1) * T])

        for b in range(ROW_BLOCKS):
            if b == M_BLOCKS:
                for k in range(J_PER_PIECE):
                    load_state(0, k)
            load_q(b, 0)
            load_scale(b)
            if b == M_BLOCKS:
                load_state(0, J_PER_PIECE)
            load_q(b, 1)
            if b == M_BLOCKS:
                load_state(0, J_PER_PIECE + 1)
        for k in range(J_BLOCKS):
            load_state(1, k)

        zeros = held.tile([P, T], BF16, name="zeros")
        nc.gpsimd.memset(zeros[:], 0.0)
        unused = flip.tile([P, T], F32, name="unused", tag="flipped")
        for i in range(WARM_UP):
            nc.tensor.matmul(unused[:], zeros[:, 0:P], zeros[:], start=True, stop=True)

        identity = held.tile([P, P], F32, name="identity")
        masks.make_identity(nc, identity[:])

        pieces = [(b, h) for b in range(ROW_BLOCKS) for h in range(PIECES)]
        centred = []

        def subtract_zero_point(u):
            b, h = pieces[u]
            tag = f"product{u - AHEAD}" if u >= AHEAD else f"centred{u}"
            tile_u = held.tile([P, PIECE], F32, name=f"centred{u}", tag=tag)
            nc.scalar.activation(tile_u[:], q_sb[b][h][:], COPY, bias=-ZERO_POINT)
            centred.append(tile_u)

        acc = {}

        def multiply(bank, weights, e, k, t0, width):
            nc.tensor.matmul(
                bank[:],
                weights,
                state_sb[e][k][:, t0 : t0 + width],
                start=(k == 0),
                stop=(k == J_BLOCKS - 1),
            )

        def copy_and_store(copy_engine, b, t0, sums_part):
            e, m_block = divmod(b, M_BLOCKS)
            width = sums_part.shape[1]
            result = held.tile([P, width], F32, name=f"result{b}_{t0}")
            if copy_engine is nc.scalar:
                nc.scalar.activation(result[:], sums_part, COPY)
            else:
                nc.vector.tensor_copy(result[:], sums_part)
            nc.sync.dma_start(
                out[m_block * P : (m_block + 1) * P, e * T + t0 : e * T + t0 + width], result[:]
            )

        last_block = ROW_BLOCKS - 1
        last_weights = []

        def copy_and_multiply(group, number):
            flipped, members = group
            width = len(members) * P
            wt_t = held.tile([P, width], BF16, name=f"wt_t{number}")
            nc.scalar.activation(wt_t[:], flipped[:, 0:width], COPY)
            for i, (b, k) in enumerate(members):
                weights = wt_t[:, i * P : (i + 1) * P]
                if b == last_block:
                    last_weights.append(weights)
                    continue
                if k == 0:
                    acc[b] = sums.tile([P, T], F32, name="acc")
                multiply(acc[b], weights, b // M_BLOCKS, k, 0, T)

        group = (flip.tile([P, PIECE], F32, name="flipped"), [])
        waiting = None
        for u in range(AHEAD):
            subtract_zero_point(u)
        for u, (b, h) in enumerate(pieces):
            wt = held.tile([P, PIECE], F32, name=f"wt{u}", tag=f"product{u}")
            nc.vector.tensor_tensor(
                wt[:],
                scale_sb[b][:].indirect(offsets[:, h * PIECE // 16 : (h + 1) * PIECE // 16]),
                centred[u][:],
                MULT,
            )

            full = group
            group = (flip.tile([P, PIECE], F32, name="flipped"), [])
            for i, (flipped, members) in enumerate([full, group]):
                place = len(members) * P
                nc.tensor.transpose(
                    flipped[:, place : place + P], wt[:, i * P : (i + 1) * P], identity[:]
                )
                members.append((b, h * J_PER_PIECE + i))
            if waiting is not None:
                copy_and_multiply(*waiting)
            waiting = (full, u)
            if u + AHEAD < len(pieces):
                subtract_zero_point(u + AHEAD)
        copy_and_multiply(*waiting)
        copy_and_multiply(group, len(pieces))

        parts = []
        t0 = 0
        for width in LAST_BANKS:
            bank = sums.tile([P, width], F32, name="acc")
            for k, weights in enumerate(last_weights):
                multiply(bank, weights, EXPERTS - 1, k, t0, width)
            parts.append((t0, bank[:]))
            t0 += width

        for b in range(last_block):
            for t0 in range(0, T, HALF):
                copy_and_store(nc.vector, b, t0, acc[b][:, t0 : t0 + HALF])
        for i, (t0, bank) in enumerate(parts):
            copy_and_store(nc.vector if i % 2 else nc.scalar, last_block, t0, bank)
